import numpy as np
import ml_dtypes

BF16 = ml_dtypes.bfloat16


def bf(x):
    return np.asarray(x, np.float32).astype(BF16)


def f32(x):
    return np.asarray(x, np.float32)


def f64(x):
    return np.asarray(x).astype(np.float64)


def striped(idx):
    return np.tile(idx.reshape(-1, 16).T, (8, 1))


V, H, P, N = 2048, 128, 512, 1024


def sigmoid(v):
    return 1.0 / (1.0 + np.exp(-v))


def setup_inputs():
    sc = 1.0 / np.sqrt(2.0 * H)
    return {"table": bf(np.random.standard_normal((H, V))), "wzl": bf(sc * np.random.standard_normal((H, H))), "wzr": bf(sc * np.random.standard_normal((H, H))), "whl": bf(sc * np.random.standard_normal((H, H))), "whr": bf(sc * np.random.standard_normal((H, H))), "bz": f32(0.2 * np.random.standard_normal((H, 1))), "bh": f32(0.2 * np.random.standard_normal((H, 1))), "offs": striped(np.random.permutation(np.tile(np.arange(V), 2))[:N])}


def reference(table, wzl, wzr, whl, whr, bz, bh, offs):
    idx = offs[:16].T.reshape(-1)
    el = f64(table)[:, idx[:P]]
    er = f64(table)[:, idx[P:]]
    z = sigmoid(f64(wzl).T @ el + f64(wzr).T @ er + f64(bz))
    ht = sigmoid(f64(whl).T @ el + f64(whr).T @ er + f64(bh))
    return (1.0 - z) * ht

@@ -1,0 +1,54 @@
+import concourse.mybir as mybir
+
+H = 128
+V = 2048
+PAIRS = 512
+LIST_COLUMNS = PAIRS // 16
+
+BF16, F32, U16 = mybir.dt.bfloat16, mybir.dt.float32, mybir.dt.uint16
+SIGMOID = mybir.ActivationFunctionType.Sigmoid
+
+FLOPS = 2 * 4 * H * H * PAIRS
+
+
+def tile_treeencoderrnn_kernel(tc, table, wzl, wzr, whl, whr, bz, bh, offs, out):
+    nc = tc.nc
+    with (
+        tc.tile_pool(name="held", bufs=1) as held,
+        tc.psum_pool(name="psum", bufs=1) as psum,
+    ):
+        offsets = held.tile([H, 2 * LIST_COLUMNS], U16, name="offsets")
+        nc.sync.dma_start(offsets[:], offs)
+        words = held.tile([H, V], BF16, name="words")
+        nc.sync.dma_start(words[:], table)
+
+        weights = {}
+        for name, source in (("wzl", wzl), ("wzr", wzr), ("whl", whl), ("whr", whr)):
+            weights[name] = held.tile([H, H], BF16, name=name)
+            nc.scalar.dma_start(weights[name][:], source)
+        bias_z = held.tile([H, 1], F32, name="bias_z")
+        nc.gpsimd.dma_start(bias_z[:], bz)
+        bias_h = held.tile([H, 1], F32, name="bias_h")
+        nc.gpsimd.dma_start(bias_h[:], bh)
+
+        minus_bias_z = held.tile([H, 1], F32, name="minus_bias_z")
+        nc.vector.tensor_scalar_mul(minus_bias_z[:], bias_z[:], -1.0)
+
+        left = words[:].indirect(offsets[:, 0:LIST_COLUMNS])
+        right = words[:].indirect(offsets[:, LIST_COLUMNS : 2 * LIST_COLUMNS])
+
+        sum_z = psum.tile([H, PAIRS], F32, name="sum_z")
+        nc.tensor.matmul(sum_z[:], weights["wzl"][:], left, start=True, stop=False)
+        nc.tensor.matmul(sum_z[:], weights["wzr"][:], right, start=False, stop=True)
+        sum_h = psum.tile([H, PAIRS], F32, name="sum_h")
+        nc.tensor.matmul(sum_h[:], weights["whl"][:], left, start=True, stop=False)
+        nc.tensor.matmul(sum_h[:], weights["whr"][:], right, start=False, stop=True)
+
+        keep = held.tile([H, PAIRS], F32, name="keep")
+        nc.scalar.activation(keep[:], sum_z[:], SIGMOID, bias=minus_bias_z[:], scale=-1.0)
+        candidate = held.tile([H, PAIRS], F32, name="candidate")
+        nc.scalar.activation(candidate[:], sum_h[:], SIGMOID, bias=bias_h[:], scale=1.0)
+
+        hidden = held.tile([H, PAIRS], F32, name="hidden")
+        nc.vector.tensor_mul(hidden[:], keep[:], candidate[:])
+        nc.sync.dma_start(out, hidden[:])

@@ -10,6 +10,8 @@ SIGMOID = mybir.ActivationFunctionType.Sigmoid
 
 FLOPS = 2 * 4 * H * H * PAIRS
 
+WARM_UP = 8
+
 
 def tile_treeencoderrnn_kernel(tc, table, wzl, wzr, whl, whr, bz, bh, offs, out):
     nc = tc.nc
@@ -17,6 +19,12 @@ def tile_treeencoderrnn_kernel(tc, table, wzl, wzr, whl, whr, bz, bh, offs, out)
         tc.tile_pool(name="held", bufs=1) as held,
         tc.psum_pool(name="psum", bufs=1) as psum,
     ):
+        zeros = held.tile([H, PAIRS], BF16, name="zeros")
+        nc.vector.memset(zeros[:], 0.0)
+        unread = psum.tile([H, PAIRS], F32, name="unread")
+        for turn in range(WARM_UP):
+            nc.tensor.matmul(unread[:], zeros[:, 0:H], zeros[:], start=True, stop=True)
+
         offsets = held.tile([H, 2 * LIST_COLUMNS], U16, name="offsets")
         nc.sync.dma_start(offsets[:], offs)
         words = held.tile([H, V], BF16, name="words")

@@ -35,9 +35,9 @@ def tile_treeencoderrnn_kernel(tc, table, wzl, wzr, whl, whr, bz, bh, offs, out)
             weights[name] = held.tile([H, H], BF16, name=name)
             nc.scalar.dma_start(weights[name][:], source)
         bias_z = held.tile([H, 1], F32, name="bias_z")
-        nc.gpsimd.dma_start(bias_z[:], bz)
+        nc.sync.dma_start(bias_z[:], bz)
         bias_h = held.tile([H, 1], F32, name="bias_h")
-        nc.gpsimd.dma_start(bias_h[:], bh)
+        nc.sync.dma_start(bias_h[:], bh)
 
         minus_bias_z = held.tile([H, 1], F32, name="minus_bias_z")
         nc.vector.tensor_scalar_mul(minus_bias_z[:], bias_z[:], -1.0)

@@ -25,6 +25,9 @@ def tile_treeencoderrnn_kernel(tc, table, wzl, wzr, whl, whr, bz, bh, offs, out)
         for turn in range(WARM_UP):
             nc.tensor.matmul(unread[:], zeros[:, 0:H], zeros[:], start=True, stop=True)
 
+        unread_sigmoid = held.tile([H, 1], F32, name="unread_sigmoid")
+        nc.scalar.activation(unread_sigmoid[:], zeros[:, 0:1], SIGMOID)
+
         offsets = held.tile([H, 2 * LIST_COLUMNS], U16, name="offsets")
         nc.sync.dma_start(offsets[:], offs)
         words = held.tile([H, V], BF16, name="words")

@@ -3,32 +3,36 @@ import concourse.mybir as mybir
 H = 128
 V = 2048
 PAIRS = 512
-LIST_COLUMNS = PAIRS // 16
+CHUNK = 256
+CHUNK_COLUMNS = CHUNK // 16
+PAIRS_COLUMNS = PAIRS // 16
 
 BF16, F32, U16 = mybir.dt.bfloat16, mybir.dt.float32, mybir.dt.uint16
 SIGMOID = mybir.ActivationFunctionType.Sigmoid
 
 FLOPS = 2 * 4 * H * H * PAIRS
 
-WARM_UP = 8
+WARM_UP = 4
 
 
 def tile_treeencoderrnn_kernel(tc, table, wzl, wzr, whl, whr, bz, bh, offs, out):
     nc = tc.nc
     with (
         tc.tile_pool(name="held", bufs=1) as held,
-        tc.psum_pool(name="psum", bufs=1) as psum,
+        tc.tile_pool(name="work", bufs=2) as work,
+        tc.psum_pool(name="unread_bank", bufs=1) as unread_bank,
+        tc.psum_pool(name="psum", bufs=2) as psum,
     ):
         zeros = held.tile([H, PAIRS], BF16, name="zeros")
         nc.vector.memset(zeros[:], 0.0)
-        unread = psum.tile([H, PAIRS], F32, name="unread")
+        unread = unread_bank.tile([H, PAIRS], F32, name="unread")
         for turn in range(WARM_UP):
             nc.tensor.matmul(unread[:], zeros[:, 0:H], zeros[:], start=True, stop=True)
 
         unread_sigmoid = held.tile([H, 1], F32, name="unread_sigmoid")
         nc.scalar.activation(unread_sigmoid[:], zeros[:, 0:1], SIGMOID)
 
-        offsets = held.tile([H, 2 * LIST_COLUMNS], U16, name="offsets")
+        offsets = held.tile([H, 2 * PAIRS_COLUMNS], U16, name="offsets")
         nc.sync.dma_start(offsets[:], offs)
         words = held.tile([H, V], BF16, name="words")
         nc.sync.dma_start(words[:], table)
@@ -45,21 +49,24 @@ def tile_treeencoderrnn_kernel(tc, table, wzl, wzr, whl, whr, bz, bh, offs, out)
         minus_bias_z = held.tile([H, 1], F32, name="minus_bias_z")
         nc.vector.tensor_scalar_mul(minus_bias_z[:], bias_z[:], -1.0)
 
-        left = words[:].indirect(offsets[:, 0:LIST_COLUMNS])
-        right = words[:].indirect(offsets[:, LIST_COLUMNS : 2 * LIST_COLUMNS])
+        for c in range(PAIRS // CHUNK):
+            first = c * CHUNK_COLUMNS
+            left = words[:].indirect(offsets[:, first : first + CHUNK_COLUMNS])
+            first = PAIRS_COLUMNS + c * CHUNK_COLUMNS
+            right = words[:].indirect(offsets[:, first : first + CHUNK_COLUMNS])
 
-        sum_z = psum.tile([H, PAIRS], F32, name="sum_z")
-        nc.tensor.matmul(sum_z[:], weights["wzl"][:], left, start=True, stop=False)
-        nc.tensor.matmul(sum_z[:], weights["wzr"][:], right, start=False, stop=True)
-        sum_h = psum.tile([H, PAIRS], F32, name="sum_h")
-        nc.tensor.matmul(sum_h[:], weights["whl"][:], left, start=True, stop=False)
-        nc.tensor.matmul(sum_h[:], weights["whr"][:], right, start=False, stop=True)
+            sum_z = psum.tile([H, CHUNK], F32, name="sum_z")
+            nc.tensor.matmul(sum_z[:], weights["wzl"][:], left, start=True, stop=False)
+            nc.tensor.matmul(sum_z[:], weights["wzr"][:], right, start=False, stop=True)
+            sum_h = psum.tile([H, CHUNK], F32, name="sum_h")
+            nc.tensor.matmul(sum_h[:], weights["whl"][:], left, start=True, stop=False)
+            nc.tensor.matmul(sum_h[:], weights["whr"][:], right, start=False, stop=True)
 
-        keep = held.tile([H, PAIRS], F32, name="keep")
-        nc.scalar.activation(keep[:], sum_z[:], SIGMOID, bias=minus_bias_z[:], scale=-1.0)
-        candidate = held.tile([H, PAIRS], F32, name="candidate")
-        nc.scalar.activation(candidate[:], sum_h[:], SIGMOID, bias=bias_h[:], scale=1.0)
+            keep = work.tile([H, CHUNK], F32, name="keep")
+            nc.scalar.activation(keep[:], sum_z[:], SIGMOID, bias=minus_bias_z[:], scale=-1.0)
+            candidate = work.tile([H, CHUNK], F32, name="candidate")
+            nc.scalar.activation(candidate[:], sum_h[:], SIGMOID, bias=bias_h[:], scale=1.0)
 
-        hidden = held.tile([H, PAIRS], F32, name="hidden")
-        nc.vector.tensor_mul(hidden[:], keep[:], candidate[:])
-        nc.sync.dma_start(out, hidden[:])
+            hidden = work.tile([H, CHUNK], F32, name="hidden")
+            nc.vector.tensor_mul(hidden[:], keep[:], candidate[:])
+            nc.sync.dma_start(out[:, c * CHUNK : (c + 1) * CHUNK], hidden[:])

@@ -4,6 +4,7 @@ H = 128
 V = 2048
 PAIRS = 512
 CHUNK = 256
+STEP = 128
 CHUNK_COLUMNS = CHUNK // 16
 PAIRS_COLUMNS = PAIRS // 16
 
@@ -20,6 +21,7 @@ def tile_treeencoderrnn_kernel(tc, table, wzl, wzr, whl, whr, bz, bh, offs, out)
     with (
         tc.tile_pool(name="held", bufs=1) as held,
         tc.tile_pool(name="work", bufs=2) as work,
+        tc.tile_pool(name="steps", bufs=PAIRS // STEP) as steps,
         tc.psum_pool(name="unread_bank", bufs=1) as unread_bank,
         tc.psum_pool(name="psum", bufs=2) as psum,
     ):
@@ -64,9 +66,11 @@ def tile_treeencoderrnn_kernel(tc, table, wzl, wzr, whl, whr, bz, bh, offs, out)
 
             keep = work.tile([H, CHUNK], F32, name="keep")
             nc.scalar.activation(keep[:], sum_z[:], SIGMOID, bias=minus_bias_z[:], scale=-1.0)
-            candidate = work.tile([H, CHUNK], F32, name="candidate")
-            nc.scalar.activation(candidate[:], sum_h[:], SIGMOID, bias=bias_h[:], scale=1.0)
-
-            hidden = work.tile([H, CHUNK], F32, name="hidden")
-            nc.vector.tensor_mul(hidden[:], keep[:], candidate[:])
-            nc.sync.dma_start(out[:, c * CHUNK : (c + 1) * CHUNK], hidden[:])
+            for first in range(0, CHUNK, STEP):
+                candidate = steps.tile([H, STEP], F32, name="candidate")
+                nc.scalar.activation(
+                    candidate[:], sum_h[:, first : first + STEP], SIGMOID, bias=bias_h[:], scale=1.0
+                )
+                hidden = steps.tile([H, STEP], F32, name="hidden")
+                nc.vector.tensor_mul(hidden[:], keep[:, first : first + STEP], candidate[:])
+                nc.sync.dma_start(out[:, c * CHUNK + first : c * CHUNK + first + STEP], hidden[:])

@@ -4,7 +4,8 @@ H = 128
 V = 2048
 PAIRS = 512
 CHUNK = 256
-STEP = 128
+STEP = 64
+STORE = 128
 CHUNK_COLUMNS = CHUNK // 16
 PAIRS_COLUMNS = PAIRS // 16
 
@@ -66,11 +67,14 @@ def tile_treeencoderrnn_kernel(tc, table, wzl, wzr, whl, whr, bz, bh, offs, out)
 
             keep = work.tile([H, CHUNK], F32, name="keep")
             nc.scalar.activation(keep[:], sum_z[:], SIGMOID, bias=minus_bias_z[:], scale=-1.0)
-            for first in range(0, CHUNK, STEP):
-                candidate = steps.tile([H, STEP], F32, name="candidate")
-                nc.scalar.activation(
-                    candidate[:], sum_h[:, first : first + STEP], SIGMOID, bias=bias_h[:], scale=1.0
-                )
-                hidden = steps.tile([H, STEP], F32, name="hidden")
-                nc.vector.tensor_mul(hidden[:], keep[:, first : first + STEP], candidate[:])
-                nc.sync.dma_start(out[:, c * CHUNK + first : c * CHUNK + first + STEP], hidden[:])
+            for half in range(0, CHUNK, STORE):
+                hidden = steps.tile([H, STORE], F32, name="hidden")
+                for first in range(half, half + STORE, STEP):
+                    candidate = steps.tile([H, STEP], F32, name="candidate")
+                    nc.scalar.activation(
+                        candidate[:], sum_h[:, first : first + STEP], SIGMOID, bias=bias_h[:], scale=1.0
+                    )
+                    nc.vector.tensor_mul(
+                        hidden[:, first - half : first - half + STEP], keep[:, first : first + STEP], candidate[:]
+                    )
+                nc.sync.dma_start(out[:, c * CHUNK + half : c * CHUNK + half + STORE], hidden[:])

@@ -5,7 +5,7 @@ V = 2048
 PAIRS = 512
 CHUNK = 256
 STEP = 64
-STORE = 128
+STORE = 256
 CHUNK_COLUMNS = CHUNK // 16
 PAIRS_COLUMNS = PAIRS // 16
 

@@ -41,7 +41,7 @@ def tile_treeencoderrnn_kernel(tc, table, wzl, wzr, whl, whr, bz, bh, offs, out)
         nc.sync.dma_start(words[:], table)
 
         weights = {}
-        for name, source in (("wzl", wzl), ("wzr", wzr), ("whl", whl), ("whr", whr)):
+        for name, source in (("wzl", wzl), ("wzr", wzr), ("whr", whr), ("whl", whl)):
             weights[name] = held.tile([H, H], BF16, name=name)
             nc.scalar.dma_start(weights[name][:], source)
         bias_z = held.tile([H, 1], F32, name="bias_z")

@@ -1,6 +1,7 @@
 import concourse.mybir as mybir
 
 H = 128
+QUARTER = H // 4
 V = 2048
 PAIRS = 512
 CHUNK = 256
@@ -45,9 +46,11 @@ def tile_treeencoderrnn_kernel(tc, table, wzl, wzr, whl, whr, bz, bh, offs, out)
             weights[name] = held.tile([H, H], BF16, name=name)
             nc.scalar.dma_start(weights[name][:], source)
         bias_z = held.tile([H, 1], F32, name="bias_z")
-        nc.sync.dma_start(bias_z[:], bz)
+        for first in range(0, H, QUARTER):
+            nc.sync.dma_start(bias_z[first : first + QUARTER], bz[first : first + QUARTER])
         bias_h = held.tile([H, 1], F32, name="bias_h")
-        nc.sync.dma_start(bias_h[:], bh)
+        for first in range(0, H, QUARTER):
+            nc.sync.dma_start(bias_h[first : first + QUARTER], bh[first : first + QUARTER])
 
         minus_bias_z = held.tile([H, 1], F32, name="minus_bias_z")
         nc.vector.tensor_scalar_mul(minus_bias_z[:], bias_z[:], -1.0)

@@ -22,9 +22,9 @@ def tile_treeencoderrnn_kernel(tc, table, wzl, wzr, whl, whr, bz, bh, offs, out)
     nc = tc.nc
     with (
         tc.tile_pool(name="held", bufs=1) as held,
-        tc.tile_pool(name="work", bufs=2) as work,
         tc.tile_pool(name="steps", bufs=PAIRS // STEP) as steps,
         tc.psum_pool(name="unread_bank", bufs=1) as unread_bank,
+        tc.psum_pool(name="psum_z", bufs=1) as psum_z,
         tc.psum_pool(name="psum", bufs=2) as psum,
     ):
         zeros = held.tile([H, PAIRS], BF16, name="zeros")
@@ -55,21 +55,27 @@ def tile_treeencoderrnn_kernel(tc, table, wzl, wzr, whl, whr, bz, bh, offs, out)
         minus_bias_z = held.tile([H, 1], F32, name="minus_bias_z")
         nc.vector.tensor_scalar_mul(minus_bias_z[:], bias_z[:], -1.0)
 
+        left = words[:].indirect(offsets[:, 0:PAIRS_COLUMNS])
+        right = words[:].indirect(offsets[:, PAIRS_COLUMNS:])
+        sum_z = psum_z.tile([H, PAIRS], F32, name="sum_z")
+        nc.tensor.matmul(sum_z[:], weights["wzl"][:], left, start=True, stop=False)
+        nc.tensor.matmul(sum_z[:], weights["wzr"][:], right, start=False, stop=True)
+        keep = held.tile([H, PAIRS], F32, name="keep")
+        for first in range(0, PAIRS, CHUNK):
+            nc.scalar.activation(
+                keep[:, first : first + CHUNK], sum_z[:, first : first + CHUNK],
+                SIGMOID, bias=minus_bias_z[:], scale=-1.0,
+            )
+
         for c in range(PAIRS // CHUNK):
             first = c * CHUNK_COLUMNS
             left = words[:].indirect(offsets[:, first : first + CHUNK_COLUMNS])
             first = PAIRS_COLUMNS + c * CHUNK_COLUMNS
             right = words[:].indirect(offsets[:, first : first + CHUNK_COLUMNS])
-
-            sum_z = psum.tile([H, CHUNK], F32, name="sum_z")
-            nc.tensor.matmul(sum_z[:], weights["wzl"][:], left, start=True, stop=False)
-            nc.tensor.matmul(sum_z[:], weights["wzr"][:], right, start=False, stop=True)
             sum_h = psum.tile([H, CHUNK], F32, name="sum_h")
             nc.tensor.matmul(sum_h[:], weights["whl"][:], left, start=True, stop=False)
             nc.tensor.matmul(sum_h[:], weights["whr"][:], right, start=False, stop=True)
 
-            keep = work.tile([H, CHUNK], F32, name="keep")
-            nc.scalar.activation(keep[:], sum_z[:], SIGMOID, bias=minus_bias_z[:], scale=-1.0)
             for half in range(0, CHUNK, STORE):
                 hidden = steps.tile([H, STORE], F32, name="hidden")
                 for first in range(half, half + STORE, STEP):
@@ -78,6 +84,6 @@ def tile_treeencoderrnn_kernel(tc, table, wzl, wzr, whl, whr, bz, bh, offs, out)
                         candidate[:], sum_h[:, first : first + STEP], SIGMOID, bias=bias_h[:], scale=1.0
                     )
                     nc.vector.tensor_mul(
-                        hidden[:, first - half : first - half + STEP], keep[:, first : first + STEP], candidate[:]
+                        hidden[:, first - half : first - half + STEP], keep[:, c * CHUNK + first : c * CHUNK + first + STEP], candidate[:]
                     )
                 nc.sync.dma_start(out[:, c * CHUNK + half : c * CHUNK + half + STORE], hidden[:])

import concourse.mybir as mybir

H = 128
QUARTER = H // 4
V = 2048
PAIRS = 512
CHUNK = 256
STEP = 64
STORE = 256
CHUNK_COLUMNS = CHUNK // 16
PAIRS_COLUMNS = PAIRS // 16

BF16, F32, U16 = mybir.dt.bfloat16, mybir.dt.float32, mybir.dt.uint16
SIGMOID = mybir.ActivationFunctionType.Sigmoid

FLOPS = 2 * 4 * H * H * PAIRS

WARM_UP = 4


def tile_treeencoderrnn_kernel(tc, table, wzl, wzr, whl, whr, bz, bh, offs, out):
    nc = tc.nc
    with (
        tc.tile_pool(name="held", bufs=1) as held,
        tc.tile_pool(name="steps", bufs=PAIRS // STEP) as steps,
        tc.psum_pool(name="unread_bank", bufs=1) as unread_bank,
        tc.psum_pool(name="psum_z", bufs=1) as psum_z,
        tc.psum_pool(name="psum", bufs=2) as psum,
    ):
        zeros = held.tile([H, PAIRS], BF16, name="zeros")
        nc.vector.memset(zeros[:], 0.0)
        unread = unread_bank.tile([H, PAIRS], F32, name="unread")
        for turn in range(WARM_UP):
            nc.tensor.matmul(unread[:], zeros[:, 0:H], zeros[:], start=True, stop=True)

        unread_sigmoid = held.tile([H, 1], F32, name="unread_sigmoid")
        nc.scalar.activation(unread_sigmoid[:], zeros[:, 0:1], SIGMOID)

        offsets = held.tile([H, 2 * PAIRS_COLUMNS], U16, name="offsets")
        nc.sync.dma_start(offsets[:], offs)
        words = held.tile([H, V], BF16, name="words")
        nc.sync.dma_start(words[:], table)

        weights = {}
        for name, source in (("wzl", wzl), ("wzr", wzr), ("whr", whr), ("whl", whl)):
            weights[name] = held.tile([H, H], BF16, name=name)
            nc.scalar.dma_start(weights[name][:], source)
        bias_z = held.tile([H, 1], F32, name="bias_z")
        for first in range(0, H, QUARTER):
            nc.sync.dma_start(bias_z[first : first + QUARTER], bz[first : first + QUARTER])
        bias_h = held.tile([H, 1], F32, name="bias_h")
        for first in range(0, H, QUARTER):
            nc.sync.dma_start(bias_h[first : first + QUARTER], bh[first : first + QUARTER])

        minus_bias_z = held.tile([H, 1], F32, name="minus_bias_z")
        nc.vector.tensor_scalar_mul(minus_bias_z[:], bias_z[:], -1.0)

        left = words[:].indirect(offsets[:, 0:PAIRS_COLUMNS])
        right = words[:].indirect(offsets[:, PAIRS_COLUMNS:])
        sum_z = psum_z.tile([H, PAIRS], F32, name="sum_z")
        nc.tensor.matmul(sum_z[:], weights["wzl"][:], left, start=True, stop=False)
        nc.tensor.matmul(sum_z[:], weights["wzr"][:], right, start=False, stop=True)
        keep = held.tile([H, PAIRS], F32, name="keep")
        for first in range(0, PAIRS, CHUNK):
            nc.scalar.activation(
                keep[:, first : first + CHUNK], sum_z[:, first : first + CHUNK],
                SIGMOID, bias=minus_bias_z[:], scale=-1.0,
            )

        for c in range(PAIRS // CHUNK):
            first = c * CHUNK_COLUMNS
            left = words[:].indirect(offsets[:, first : first + CHUNK_COLUMNS])
            first = PAIRS_COLUMNS + c * CHUNK_COLUMNS
            right = words[:].indirect(offsets[:, first : first + CHUNK_COLUMNS])
            sum_h = psum.tile([H, CHUNK], F32, name="sum_h")
            nc.tensor.matmul(sum_h[:], weights["whl"][:], left, start=True, stop=False)
            nc.tensor.matmul(sum_h[:], weights["whr"][:], right, start=False, stop=True)

            for half in range(0, CHUNK, STORE):
                hidden = steps.tile([H, STORE], F32, name="hidden")
                for first in range(half, half + STORE, STEP):
                    candidate = steps.tile([H, STEP], F32, name="candidate")
                    nc.scalar.activation(
                        candidate[:], sum_h[:, first : first + STEP], SIGMOID, bias=bias_h[:], scale=1.0
                    )
                    nc.vector.tensor_mul(
                        hidden[:, first - half : first - half + STEP], keep[:, c * CHUNK + first : c * CHUNK + first + STEP], candidate[:]
                    )
                nc.sync.dma_start(out[:, c * CHUNK + half : c * CHUNK + half + STORE], hidden[:])
